import numpy as np
import ml_dtypes


def mxq(x, axis, fmt="e4m3"):
    dtype, down = {"e4m3": (ml_dtypes.float8_e4m3fn, 7), "e5m2": (ml_dtypes.float8_e5m2, 14)}[fmt]
    v = np.moveaxis(np.asarray(x, np.float32).astype(ml_dtypes.bfloat16).astype(np.float64), axis, -1)
    blocks = v.reshape(v.shape[:-1] + (-1, 32))
    amax = np.abs(blocks).max(-1, keepdims=True)
    byte = np.maximum(np.where(amax > 0, np.frexp(amax)[1] - 1 + 127, 0) - down, 1)
    scale = np.exp2(byte - 127.0)
    codes = (blocks / scale).astype(np.float32).astype(dtype).astype(np.float64)
    return np.moveaxis((codes * scale).reshape(v.shape), -1, axis)


WIDE = False


def mx_kscale(k):
    if not WIDE:
        return np.ones(k)
    levels = np.array([10, -10, 5, -5, 0])
    if k % 512:
        return np.exp2(np.random.permutation(np.resize(levels, k // 32))).repeat(32)
    a = np.empty((k // 512, 16))
    for p in range(k // 512):
        a[p, :8] = np.random.permutation(np.resize(levels, 8))
        for g in range(8):
            far = levels[np.abs(levels - a[p, g]) >= 10]
            a[p, g + 8] = far[np.random.randint(len(far))]
    return np.exp2(a.ravel()).repeat(32)


BF16 = ml_dtypes.bfloat16


def bf(x):
    return np.asarray(x, np.float32).astype(BF16)


def f64(x):
    return np.asarray(x).astype(np.float64)


B, H, W, C, F, K, G, RR = 4, 32, 32, 1024, 256, 3, 16, 4
KK = K * K
P = B * H * W


def setup_inputs():
    s = mx_kscale(C)
    return {"x": bf(np.random.standard_normal((B, H, W, C)) * s),
            "Wi": bf(np.random.standard_normal((C, F)) / np.sqrt(C) / s[:, None]),
            "bi": bf(np.random.standard_normal(F) * 0.3),
            "w_span": bf(np.random.standard_normal((B, H, W, KK * G)) * 0.7)}


def core(x, Wi, bi, w_span):
    xi = ((mxq(f64(x).reshape(P, C), 1, "e4m3") @ mxq(f64(Wi), 0, "e4m3")) + f64(bi)).reshape(B, H, W, F)
    pad = (K - 1) // 2
    xp = np.pad(xi, ((0, 0), (pad, pad), (pad, pad), (0, 0)))
    patches = np.stack([xp[:, i:i + H, j:j + W, :] for i in range(K) for j in range(K)], axis=-2)
    patches = patches.reshape(B, H, W, G, F // G, KK)
    w = f64(w_span).reshape(B, H, W, G, KK)[:, :, :, :, None, :]
    return (w * patches).sum(-1).reshape(B, H, W, F)


def e4m3fn_bytes(y):
    return np.clip(np.asarray(y, np.float64), -448.0, 448.0).astype(np.float32).astype(ml_dtypes.float8_e4m3fn).view(np.uint8)


def reference(x, Wi, bi, w_span):
    out = core(x, Wi, bi, w_span)
    s = np.max(np.abs(out)) / 448.0
    return out, e4m3fn_bytes(out / s)

@@ -1,0 +1,284 @@
+from contextlib import ExitStack
+
+import concourse.mybir as mybir
+from concourse.masks import make_identity
+
+F32 = mybir.dt.float32
+BF16 = mybir.dt.bfloat16
+U32 = mybir.dt.uint32
+U8 = mybir.dt.uint8
+FP8X4 = mybir.dt.float8_e4m3fn_x4
+FP8 = mybir.dt.float8_e4m3fn
+ALU = mybir.AluOpType
+ACT = mybir.ActivationFunctionType
+AX = mybir.AxisListType
+
+P = 128
+NV = 32
+C = 1024
+F = 256
+Q = 144
+FLOPS = 2 * 4096 * 1024 * 256 + 2 * 4096 * 2304
+
+RING = 16
+BLK = 130
+CHUNKS = [(0, 2), (2, 2)] + [(v, 4) for v in range(4, NV, 4)]
+AHEAD = 6
+UNITS = [(0, 4, 0, 3), (3, 4, 3, 3), (6, 3, 6, 2), (9, 4, 8, 3), (12, 4, 11, 3), (15, 3, 14, 2)]
+V_UNITS = (2, 5)
+V_UNITS_LAST = (1, 2, 4, 5)
+S_SUBS = (2, 5, 7)
+
+
+def tile_involution2d_pa_kernel(tc, x, Wi, bi, w_span, out_0, out_1):
+    nc = tc.nc
+    xv = x.rearrange("b u v k -> (b u) v k")
+    wv = w_span.rearrange("b u v q -> (b u) (v q)")
+    o0 = out_0.rearrange("b u v c -> (b u) v c")
+    o1 = out_1.rearrange("b u v c -> (b u) (v c)")
+
+
+    with ExitStack() as ctx:
+        const = ctx.enter_context(tc.tile_pool(name="const", bufs=1))
+        xpool = ctx.enter_context(tc.tile_pool(name="xpool", bufs=3))
+        gpool = ctx.enter_context(tc.tile_pool(name="gpool", bufs=2))
+        cpool = ctx.enter_context(tc.tile_pool(name="cpool", bufs=2))
+        ppool = ctx.enter_context(tc.tile_pool(name="ppool", bufs=3))
+        fpool = ctx.enter_context(tc.tile_pool(name="fpool", bufs=4))
+        psx = ctx.enter_context(tc.psum_pool(name="psx", bufs=2))
+        psa = ctx.enter_context(tc.psum_pool(name="psa", bufs=2))
+        psp = ctx.enter_context(tc.psum_pool(name="psp", bufs=4))
+
+        xtiles = {}
+
+        def load_chunk(k):
+            v0, nv = CHUNKS[k]
+            x_sb = xpool.tile([P, nv, C], BF16, tag="x", name="x_sb")
+            nc.sync.dma_start(out=x_sb[:], in_=xv[:, v0:v0 + nv, :])
+            xtiles[k] = x_sb
+
+        load_chunk(0)
+        wi_raw = const.tile([P, 2, 4, F], BF16)
+        nc.sync.dma_start(out=wi_raw[:], in_=Wi.rearrange("(g p j) c -> p g j c", g=2, j=4))
+        bias = []
+        for h in range(2):
+            b_h = const.tile([P, 1], BF16, name="bias%d" % h)
+            nc.sync.dma_start(out=b_h[:], in_=bi[128 * h:128 * (h + 1)].rearrange("(p o) -> p o", o=1))
+            bias.append(b_h)
+        load_chunk(1)
+        w_all = const.tile([P, NV * Q], BF16)
+        nc.sync.dma_start(out=w_all[:], in_=wv)
+        load_chunk(2)
+
+        ident = const.tile([P, P], F32)
+        make_identity(nc, ident[:])
+        zblk = const.tile([P, P], F32)
+        nc.gpsimd.memset(zblk[:], 0.0)
+        zcol = const.tile([P, 1], F32)
+        nc.gpsimd.memset(zcol[:], 0.0)
+        ring = []
+        for i in range(3):
+            row = []
+            for h in range(2):
+                r_ih = const.tile([P, RING, BLK], F32, name="ring%d%d" % (i, h))
+                if i == 0:
+                    nc.gpsimd.memset(r_ih[:, :, 0:129:32], 0.0)
+                if i == 2:
+                    nc.gpsimd.memset(r_ih[:, :, 1:130:32], 0.0)
+                row.append(r_ih)
+            ring.append(row)
+        out_keep = const.tile([P, NV, F], F32)
+        pm = const.tile([P, NV], F32)
+
+        wi_grp = const.tile([P, 2, F, 4], BF16, align_bytes=64)
+        nc.vector.tensor_copy(out=wi_grp[:], in_=wi_raw[:].rearrange("p g j c -> p g c j"))
+        wi_codes = const.tile([P, 2 * F], U32, align_bytes=64)
+        wi_scales = const.tile([P, 2 * F], U8, align_bytes=64)
+        nc.vector.quantize_mx(
+            out=wi_codes[:].bitcast(FP8X4),
+            scales=wi_scales[:],
+            in_=wi_grp[:].rearrange("p g c j -> p (g c j)"),
+        )
+
+        grps = {}
+
+        def turn(k, r):
+            v0, nv = CHUNKS[k]
+            if r == 0:
+                grp_new = gpool.tile([P, 2, nv * P, 2], F32, tag="grp", name="grp", align_bytes=64)
+                grps[k] = grp_new
+                if k + 2 < len(CHUNKS) and k >= 1:
+                    load_chunk(k + 2)
+            grp = grps[k]
+            words = xtiles[k][:, r, :].bitcast(F32)
+            xt = psx.tile([P, 2, 2, P], F32, tag="xt", name="xt")
+            for g in range(2):
+                for u in range(2):
+                    nc.tensor.transpose(xt[:, g, u, :], words[:, 256 * g + u:256 * (g + 1):2], ident[:])
+            nc.scalar.copy(out=grp[:, :, r * P:(r + 1) * P, :], in_=xt[:].rearrange("p g u r -> p g r u"))
+
+        def project(k):
+            v0, nv = CHUNKS[k]
+            n = nv * P
+            codes = cpool.tile([P, 2 * n], U32, tag="codes", name="codes", align_bytes=64)
+            scal = cpool.tile([P, 2 * n], U8, tag="scal", name="scal", align_bytes=64)
+            nc.vector.quantize_mx(
+                out=codes[:].bitcast(FP8X4),
+                scales=scal[:],
+                in_=grps[k][:].rearrange("p g r u -> p (g r u)").bitcast(BF16),
+            )
+            s0 = v0 % RING
+            for h in range(2):
+                acc = psa.tile([P, n], F32, tag="acc", name="acc")
+                for g in range(2):
+                    wc = slice(g * F + h * P, g * F + (h + 1) * P)
+                    xc = slice(g * n, (g + 1) * n)
+                    nc.tensor.matmul_mx(
+                        out=acc[:],
+                        lhsT=wi_codes[:, wc].bitcast(FP8X4),
+                        lhsT_scale=wi_scales[:, wc],
+                        rhs=codes[:, xc].bitcast(FP8X4),
+                        rhs_scale=scal[:, xc],
+                        start=(g == 0),
+                        stop=(g == 1),
+                    )
+                a3 = acc[:].rearrange("p (s e) -> p s e", e=P)
+                a4 = acc[:].rearrange("p (s b u) -> p s b u", b=4, u=32)
+                nc.scalar.activation(out=ring[1][h][:, s0:s0 + nv, 1:129], in_=a3, func=ACT.Identity,
+                                     bias=bias[h][:, 0:1])
+                d0 = ring[0][h][:, s0:s0 + nv, 1:129].rearrange("p s (b u) -> p s b u", u=32)
+                nc.scalar.activation(out=d0[:, :, :, 0:31], in_=a4[:, :, :, 0:31], func=ACT.Identity,
+                                     bias=bias[h][:, 0:1])
+                d2 = ring[2][h][:, s0:s0 + nv, 1:129].rearrange("p s (b u) -> p s b u", u=32)
+                nc.scalar.activation(out=d2[:, :, :, 1:32], in_=a4[:, :, :, 1:32], func=ACT.Identity,
+                                     bias=bias[h][:, 0:1])
+
+        steps = []
+        last_step = {}
+        for k, chunk in enumerate(CHUNKS):
+            for r in range(chunk[1]):
+                steps.append((0, k, r))
+                last_step[chunk[0] + r] = len(steps)
+            steps.append((1, k, 0))
+            last_step[chunk[0] + chunk[1] - 1] = len(steps)
+        done = [0]
+
+        def advance(v):
+            goal = last_step[min(v, NV - 1)]
+            while done[0] < goal:
+                kind, k, r = steps[done[0]]
+                if kind == 0:
+                    turn(k, r)
+                else:
+                    project(k)
+                done[0] += 1
+
+        def involve(v):
+            v_units = V_UNITS_LAST if v == NV - 1 else V_UNITS
+            g_groups = []
+            for ui, unit in enumerate(UNITS):
+                if ui not in v_units:
+                    g_groups.extend(range(unit[2], unit[2] + unit[3]))
+            ng_all = 16 * len(g_groups)
+            runs = []
+            for pos, g in enumerate(g_groups):
+                if runs and runs[-1][1] + runs[-1][2] == g:
+                    runs[-1][2] += 1
+                else:
+                    runs.append([pos, g, 1])
+            prod_g = ppool.tile([P, 9, ng_all], F32, tag="prod_g", name="prod_g")
+            for ui, unit in enumerate(UNITS):
+                tau0, ntau, g0, ng = unit
+                bank = psp.tile([P, 512], F32, tag="bank", name="bank")
+                for k in range(ntau):
+                    t, h = divmod(tau0 + k, 2)
+                    i, j = divmod(t, 3)
+                    vp = v + j - 1
+                    if 0 <= vp < NV:
+                        src = ring[i][h][:, vp % RING, i:i + P]
+                    else:
+                        src = zblk[:]
+                    nc.tensor.transpose(bank[:, k * P:(k + 1) * P], src, ident[:])
+                off = Q * g0 - P * tau0
+                pv = bank[:, off:off + Q * ng]
+                wsl = w_all[:, Q * v + 9 * g0:Q * v + 9 * (g0 + ng)]
+                if ui in v_units:
+                    prod_v = ppool.tile([P, ng, 16, 9], F32, tag="prod_v", name="prod_v")
+                    nc.vector.tensor_tensor(
+                        out=prod_v[:],
+                        in0=pv.rearrange("p (g j m) -> p g j m", j=16, m=9),
+                        in1=wsl.rearrange("p (g m) -> p g m", m=9).unsqueeze(2).to_broadcast([P, ng, 16, 9]),
+                        op=ALU.mult,
+                    )
+                    nc.vector.tensor_reduce(
+                        out=out_keep[:, v, 16 * g0:16 * (g0 + ng)],
+                        in_=prod_v[:].rearrange("p g j m -> p (g j) m"),
+                        axis=AX.X,
+                        op=ALU.add,
+                    )
+                else:
+                    c0 = 16 * g_groups.index(g0)
+                    nc.vector.tensor_tensor(
+                        out=prod_g[:, :, c0:c0 + 16 * ng].rearrange("p m (g j) -> p m g j", j=16),
+                        in0=pv.rearrange("p (g j m) -> p m g j", j=16, m=9),
+                        in1=wsl.rearrange("p (g m) -> p m g", m=9).unsqueeze(3).to_broadcast([P, 9, ng, 16]),
+                        op=ALU.mult,
+                    )
+            nc.gpsimd.tensor_tensor(out=prod_g[:, 0:4, :], in0=prod_g[:, 0:4, :], in1=prod_g[:, 4:8, :], op=ALU.add)
+            nc.gpsimd.tensor_tensor(out=prod_g[:, 0:2, :], in0=prod_g[:, 0:2, :], in1=prod_g[:, 2:4, :], op=ALU.add)
+            nc.gpsimd.tensor_tensor(out=prod_g[:, 0, :], in0=prod_g[:, 0, :], in1=prod_g[:, 1, :], op=ALU.add)
+            if len(runs) == 2 and runs[0][2] == runs[1][2] and runs[0][1] == 0 and runs[1][1] == 8:
+                wid = 16 * runs[0][2]
+                nc.gpsimd.tensor_tensor(
+                    out=out_keep[:, v, :].rearrange("p (a c) -> p a c", a=2)[:, :, 0:wid],
+                    in0=prod_g[:, 0, :].rearrange("p (a c) -> p a c", a=2),
+                    in1=prod_g[:, 8, :].rearrange("p (a c) -> p a c", a=2),
+                    op=ALU.add,
+                )
+            else:
+                for pos, g, cnt in runs:
+                    nc.gpsimd.tensor_tensor(
+                        out=out_keep[:, v, 16 * g:16 * (g + cnt)],
+                        in0=prod_g[:, 0, 16 * pos:16 * (pos + cnt)],
+                        in1=prod_g[:, 8, 16 * pos:16 * (pos + cnt)],
+                        op=ALU.add,
+                    )
+
+        def finish(v):
+            nc.vector.tensor_reduce(out=pm[:, v:v + 1], in_=out_keep[:, v, :], axis=AX.X, op=ALU.max,
+                                    apply_absolute_value=True)
+            nc.sync.dma_start(out=o0[:, v, :], in_=out_keep[:, v, :])
+
+        advance(AHEAD - 1)
+        for v in range(NV):
+            advance(v + AHEAD)
+            involve(v)
+            if v >= 2:
+                finish(v - 2)
+        finish(NV - 2)
+        finish(NV - 1)
+
+        pmax = const.tile([P, 1], F32)
+        nc.vector.tensor_reduce(out=pmax[:], in_=pm[:], axis=AX.X, op=ALU.max)
+        spread = psx.tile([P, P], F32, tag="xt", name="spread")
+        nc.tensor.transpose(spread[:], pmax[:, 0:1].to_broadcast([P, P]), ident[:])
+        amax = const.tile([P, 1], F32)
+        nc.vector.tensor_reduce(out=amax[:], in_=spread[:], axis=AX.X, op=ALU.max)
+        rec = const.tile([P, 1], F32)
+        nc.vector.reciprocal(out=rec[:], in_=amax[:])
+        fac = const.tile([P, 1], F32)
+        nc.vector.tensor_scalar(out=fac[:], in0=rec[:], scalar1=448.0, scalar2=None, op0=ALU.mult)
+
+        flat = out_keep[:].rearrange("p v c -> p (v c)")
+        for piece in range(4):
+            f8 = fpool.tile([P, 2048], FP8, tag="f8", name="f8")
+            for sub in range(4):
+                a = 512 * sub
+                b = 2048 * piece + a
+                if (4 * piece + sub) % 8 in S_SUBS:
+                    nc.scalar.activation(out=f8[:, a:a + 512], in_=flat[:, b:b + 512], func=ACT.Identity,
+                                         scale=fac[:, 0:1], bias=zcol[:, 0:1], saturate=False)
+                else:
+                    nc.vector.tensor_scalar(out=f8[:, a:a + 512], in0=flat[:, b:b + 512], scalar1=fac[:, 0:1],
+                                            scalar2=None, op0=ALU.mult, saturate=False)
+            nc.sync.dma_start(out=o1[:, 2048 * piece:2048 * (piece + 1)], in_=f8[:].bitcast(U8))

@@ -20,13 +20,12 @@ F = 256
 Q = 144
 FLOPS = 2 * 4096 * 1024 * 256 + 2 * 4096 * 2304
 
-RING = 16
+XR = 12
 BLK = 130
+R = 16
 CHUNKS = [(0, 2), (2, 2)] + [(v, 4) for v in range(4, NV, 4)]
-AHEAD = 6
-UNITS = [(0, 4, 0, 3), (3, 4, 3, 3), (6, 3, 6, 2), (9, 4, 8, 3), (12, 4, 11, 3), (15, 3, 14, 2)]
-V_UNITS = (2, 5)
-V_UNITS_LAST = (1, 2, 4, 5)
+AHEAD = 8
+LOOK = 2
 S_SUBS = (2, 5, 7)
 
 
@@ -37,7 +36,6 @@ def tile_involution2d_pa_kernel(tc, x, Wi, bi, w_span, out_0, out_1):
     o0 = out_0.rearrange("b u v c -> (b u) v c")
     o1 = out_1.rearrange("b u v c -> (b u) (v c)")
 
-
     with ExitStack() as ctx:
         const = ctx.enter_context(tc.tile_pool(name="const", bufs=1))
         xpool = ctx.enter_context(tc.tile_pool(name="xpool", bufs=3))
@@ -47,7 +45,8 @@ def tile_involution2d_pa_kernel(tc, x, Wi, bi, w_span, out_0, out_1):
         fpool = ctx.enter_context(tc.tile_pool(name="fpool", bufs=4))
         psx = ctx.enter_context(tc.psum_pool(name="psx", bufs=2))
         psa = ctx.enter_context(tc.psum_pool(name="psa", bufs=2))
-        psp = ctx.enter_context(tc.psum_pool(name="psp", bufs=4))
+        pst = ctx.enter_context(tc.psum_pool(name="pst", bufs=1))
+        psw = ctx.enter_context(tc.psum_pool(name="psw", bufs=2))
 
         xtiles = {}
 
@@ -72,23 +71,24 @@ def tile_involution2d_pa_kernel(tc, x, Wi, bi, w_span, out_0, out_1):
 
         ident = const.tile([P, P], F32)
         make_identity(nc, ident[:])
-        zblk = const.tile([P, P], F32)
-        nc.gpsimd.memset(zblk[:], 0.0)
+        ident_bf = const.tile([P, P], BF16)
+        make_identity(nc, ident_bf[:])
         zcol = const.tile([P, 1], F32)
         nc.gpsimd.memset(zcol[:], 0.0)
-        ring = []
-        for i in range(3):
-            row = []
-            for h in range(2):
-                r_ih = const.tile([P, RING, BLK], F32, name="ring%d%d" % (i, h))
-                if i == 0:
-                    nc.gpsimd.memset(r_ih[:, :, 0:129:32], 0.0)
-                if i == 2:
-                    nc.gpsimd.memset(r_ih[:, :, 1:130:32], 0.0)
-                row.append(r_ih)
-            ring.append(row)
-        out_keep = const.tile([P, NV, F], F32)
+        x_t = []
+        for h in range(2):
+            t_h = const.tile([P, XR, BLK], F32, name="x_t%d" % h)
+            nc.gpsimd.memset(t_h[:, :, 0:BLK:BLK - 1], 0.0)
+            x_t.append(t_h)
+        xp = const.tile([P, 3, R + 2, F], F32)
+        nc.gpsimd.memset(xp[:, :, 0, :], 0.0)
+        out_keep = const.tile([P, NV * F], F32)
         pm = const.tile([P, NV], F32)
+        msum = const.tile([P, 2], F32)
+        nc.vector.tensor_reduce(out=msum[:, 0:1], in_=ident[:, 0:P:32], axis=AX.X, op=ALU.add)
+        nc.vector.tensor_reduce(out=msum[:, 1:2], in_=ident[:, 31:P:32], axis=AX.X, op=ALU.add)
+        mask = const.tile([P, 2], F32)
+        nc.vector.tensor_scalar(out=mask[:], in0=msum[:], scalar1=-1.0, scalar2=1.0, op0=ALU.mult, op1=ALU.add)
 
         wi_grp = const.tile([P, 2, F, 4], BF16, align_bytes=64)
         nc.vector.tensor_copy(out=wi_grp[:], in_=wi_raw[:].rearrange("p g j c -> p g c j"))
@@ -103,7 +103,7 @@ def tile_involution2d_pa_kernel(tc, x, Wi, bi, w_span, out_0, out_1):
         grps = {}
 
         def turn(k, r):
-            v0, nv = CHUNKS[k]
+            nv = CHUNKS[k][1]
             if r == 0:
                 grp_new = gpool.tile([P, 2, nv * P, 2], F32, tag="grp", name="grp", align_bytes=64)
                 grps[k] = grp_new
@@ -127,7 +127,7 @@ def tile_involution2d_pa_kernel(tc, x, Wi, bi, w_span, out_0, out_1):
                 scales=scal[:],
                 in_=grps[k][:].rearrange("p g r u -> p (g r u)").bitcast(BF16),
             )
-            s0 = v0 % RING
+            s0 = v0 % XR
             for h in range(2):
                 acc = psa.tile([P, n], F32, tag="acc", name="acc")
                 for g in range(2):
@@ -142,16 +142,8 @@ def tile_involution2d_pa_kernel(tc, x, Wi, bi, w_span, out_0, out_1):
                         start=(g == 0),
                         stop=(g == 1),
                     )
-                a3 = acc[:].rearrange("p (s e) -> p s e", e=P)
-                a4 = acc[:].rearrange("p (s b u) -> p s b u", b=4, u=32)
-                nc.scalar.activation(out=ring[1][h][:, s0:s0 + nv, 1:129], in_=a3, func=ACT.Identity,
-                                     bias=bias[h][:, 0:1])
-                d0 = ring[0][h][:, s0:s0 + nv, 1:129].rearrange("p s (b u) -> p s b u", u=32)
-                nc.scalar.activation(out=d0[:, :, :, 0:31], in_=a4[:, :, :, 0:31], func=ACT.Identity,
-                                     bias=bias[h][:, 0:1])
-                d2 = ring[2][h][:, s0:s0 + nv, 1:129].rearrange("p s (b u) -> p s b u", u=32)
-                nc.scalar.activation(out=d2[:, :, :, 1:32], in_=a4[:, :, :, 1:32], func=ACT.Identity,
-                                     bias=bias[h][:, 0:1])
+                nc.scalar.activation(out=x_t[h][:, s0:s0 + nv, 1:1 + P], in_=acc[:].rearrange("p (s e) -> p s e", e=P),
+                                     func=ACT.Identity, bias=bias[h][:, 0:1])
 
         steps = []
         last_step = {}
@@ -173,88 +165,110 @@ def tile_involution2d_pa_kernel(tc, x, Wi, bi, w_span, out_0, out_1):
                     project(k)
                 done[0] += 1
 
+        def slots_of(v2):
+            found = []
+            for v in (v2 - 2, v2 - 1, v2):
+                if 0 <= v < NV:
+                    s = v % R + v2 - v
+                    if s not in found:
+                        found.append(s)
+            return found
+
+        def to_pixels(vp):
+            pta = pst.tile([P, 2, F], F32, tag="pta", name="pta")
+            ptb = pst.tile([P, F], F32, tag="ptb", name="ptb")
+            parts = [pta[:, 0, :], pta[:, 1, :], ptb[:]]
+            for i in range(3):
+                for h in range(2):
+                    nc.tensor.transpose(parts[i][:, h * P:(h + 1) * P], x_t[h][:, vp % XR, i:i + P], ident[:])
+            for s in slots_of(vp + 1):
+                nc.scalar.activation(out=xp[:, 0, s, :], in_=parts[0], func=ACT.Copy, scale=mask[:, 0:1])
+                nc.scalar.copy(out=xp[:, 1, s, :], in_=parts[1])
+                nc.scalar.activation(out=xp[:, 2, s, :], in_=parts[2], func=ACT.Copy, scale=mask[:, 1:2])
+
+        wtiles = {}
+        cuts = {}
+        prods = {}
+
+        def weights(v):
+            wps = psw.tile([P, 90], F32, tag="wps", name="wps")
+            nc.tensor.matmul(out=wps[:], lhsT=ident_bf[:], rhs=w_all[:, Q * v + 45:Q * v + 135], start=True, stop=True)
+            wtiles[v] = wps
+
+        def cut_groups(v):
+            base = v % R
+            cut = ppool.tile([P, 2, Q], F32, tag="cut", name="cut")
+            nc.scalar.copy(out=cut[:, 0, 0:48], in_=xp[:, 0, base + 2, 208:256])
+            nc.scalar.copy(out=cut[:, 0, 48:144], in_=xp[:, 1, base, 0:96])
+            nc.scalar.copy(out=cut[:, 1, 0:96], in_=xp[:, 1, base + 2, 160:256])
+            nc.scalar.copy(out=cut[:, 1, 96:144], in_=xp[:, 2, base, 0:48])
+            cuts[v] = cut
+
         def involve(v):
-            v_units = V_UNITS_LAST if v == NV - 1 else V_UNITS
-            g_groups = []
-            for ui, unit in enumerate(UNITS):
-                if ui not in v_units:
-                    g_groups.extend(range(unit[2], unit[2] + unit[3]))
-            ng_all = 16 * len(g_groups)
-            runs = []
-            for pos, g in enumerate(g_groups):
-                if runs and runs[-1][1] + runs[-1][2] == g:
-                    runs[-1][2] += 1
-                else:
-                    runs.append([pos, g, 1])
-            prod_g = ppool.tile([P, 9, ng_all], F32, tag="prod_g", name="prod_g")
-            for ui, unit in enumerate(UNITS):
-                tau0, ntau, g0, ng = unit
-                bank = psp.tile([P, 512], F32, tag="bank", name="bank")
-                for k in range(ntau):
-                    t, h = divmod(tau0 + k, 2)
-                    i, j = divmod(t, 3)
-                    vp = v + j - 1
-                    if 0 <= vp < NV:
-                        src = ring[i][h][:, vp % RING, i:i + P]
-                    else:
-                        src = zblk[:]
-                    nc.tensor.transpose(bank[:, k * P:(k + 1) * P], src, ident[:])
-                off = Q * g0 - P * tau0
-                pv = bank[:, off:off + Q * ng]
-                wsl = w_all[:, Q * v + 9 * g0:Q * v + 9 * (g0 + ng)]
-                if ui in v_units:
-                    prod_v = ppool.tile([P, ng, 16, 9], F32, tag="prod_v", name="prod_v")
-                    nc.vector.tensor_tensor(
-                        out=prod_v[:],
-                        in0=pv.rearrange("p (g j m) -> p g j m", j=16, m=9),
-                        in1=wsl.rearrange("p (g m) -> p g m", m=9).unsqueeze(2).to_broadcast([P, ng, 16, 9]),
-                        op=ALU.mult,
-                    )
-                    nc.vector.tensor_reduce(
-                        out=out_keep[:, v, 16 * g0:16 * (g0 + ng)],
-                        in_=prod_v[:].rearrange("p g j m -> p (g j) m"),
-                        axis=AX.X,
-                        op=ALU.add,
-                    )
-                else:
-                    c0 = 16 * g_groups.index(g0)
-                    nc.vector.tensor_tensor(
-                        out=prod_g[:, :, c0:c0 + 16 * ng].rearrange("p m (g j) -> p m g j", j=16),
-                        in0=pv.rearrange("p (g j m) -> p m g j", j=16, m=9),
-                        in1=wsl.rearrange("p (g m) -> p m g", m=9).unsqueeze(3).to_broadcast([P, 9, ng, 16]),
-                        op=ALU.mult,
-                    )
-            nc.gpsimd.tensor_tensor(out=prod_g[:, 0:4, :], in0=prod_g[:, 0:4, :], in1=prod_g[:, 4:8, :], op=ALU.add)
-            nc.gpsimd.tensor_tensor(out=prod_g[:, 0:2, :], in0=prod_g[:, 0:2, :], in1=prod_g[:, 2:4, :], op=ALU.add)
-            nc.gpsimd.tensor_tensor(out=prod_g[:, 0, :], in0=prod_g[:, 0, :], in1=prod_g[:, 1, :], op=ALU.add)
-            if len(runs) == 2 and runs[0][2] == runs[1][2] and runs[0][1] == 0 and runs[1][1] == 8:
-                wid = 16 * runs[0][2]
+            base = v % R
+            wps = wtiles[v]
+            prod = ppool.tile([P, 16, 16, 9], F32, tag="prod", name="prod")
+            rows = [xp[:, i, base:base + 3, :].rearrange("p s c -> p (s c)") for i in range(3)]
+
+            def on_gpsimd(g0, n, src):
                 nc.gpsimd.tensor_tensor(
-                    out=out_keep[:, v, :].rearrange("p (a c) -> p a c", a=2)[:, :, 0:wid],
-                    in0=prod_g[:, 0, :].rearrange("p (a c) -> p a c", a=2),
-                    in1=prod_g[:, 8, :].rearrange("p (a c) -> p a c", a=2),
-                    op=ALU.add,
+                    out=prod[:, g0:g0 + n, :, :],
+                    in0=src.rearrange("p (g j m) -> p g j m", j=16, m=9),
+                    in1=w_all[:, Q * v + 9 * g0:Q * v + 9 * (g0 + n)].rearrange("p (g m) -> p g m", m=9).unsqueeze(
+                        2).to_broadcast([P, n, 16, 9]),
+                    op=ALU.mult,
                 )
-            else:
-                for pos, g, cnt in runs:
-                    nc.gpsimd.tensor_tensor(
-                        out=out_keep[:, v, 16 * g:16 * (g + cnt)],
-                        in0=prod_g[:, 0, 16 * pos:16 * (pos + cnt)],
-                        in1=prod_g[:, 8, 16 * pos:16 * (pos + cnt)],
-                        op=ALU.add,
-                    )
+
+            on_gpsimd(0, 5, rows[0][:, 0:5 * Q])
+            on_gpsimd(11, 5, rows[2][:, 48:48 + 5 * Q])
+            on_gpsimd(6, 2, rows[1][:, 96:96 + 2 * Q])
+            nc.vector.tensor_tensor(
+                out=prod[:, 8:10, :, :],
+                in0=rows[1][:, 96 + 2 * Q:96 + 4 * Q].rearrange("p (g j m) -> p g j m", j=16, m=9),
+                in1=wps[:, 27:45].rearrange("p (g m) -> p g m", m=9).unsqueeze(2).to_broadcast([P, 2, 16, 9]),
+                op=ALU.mult,
+            )
+            nc.vector.tensor_tensor(
+                out=prod[:, 5:11:5, :, :],
+                in0=cuts[v][:].rearrange("p g (j m) -> p g j m", m=9),
+                in1=wps[:].rearrange("p (g r) -> p g r", r=45)[:, :, 0:9].unsqueeze(2).to_broadcast([P, 2, 16, 9]),
+                op=ALU.mult,
+            )
+            prods[v] = prod
+
+        def reduce_nine(v):
+            nc.vector.tensor_reduce(
+                out=out_keep[:, F * v:F * (v + 1)],
+                in_=prods[v][:].rearrange("p g j m -> p (g j) m"),
+                axis=AX.X,
+                op=ALU.add,
+            )
 
         def finish(v):
-            nc.vector.tensor_reduce(out=pm[:, v:v + 1], in_=out_keep[:, v, :], axis=AX.X, op=ALU.max,
+            nc.vector.tensor_reduce(out=pm[:, v:v + 1], in_=out_keep[:, F * v:F * (v + 1)], axis=AX.X, op=ALU.max,
                                     apply_absolute_value=True)
-            nc.sync.dma_start(out=o0[:, v, :], in_=out_keep[:, v, :])
+            nc.sync.dma_start(out=o0[:, v, :], in_=out_keep[:, F * v:F * (v + 1)])
 
-        advance(AHEAD - 1)
+        advance(3)
+        for vp in range(LOOK + 1):
+            to_pixels(vp)
+        weights(0)
+        cut_groups(0)
         for v in range(NV):
             advance(v + AHEAD)
+            if v + 1 + LOOK < NV:
+                to_pixels(v + 1 + LOOK)
+            if v == NV - 4:
+                nc.gpsimd.memset(xp[:, :, R + 1, :], 0.0)
+            if v + 1 < NV:
+                weights(v + 1)
+                cut_groups(v + 1)
             involve(v)
+            if v >= 1:
+                reduce_nine(v - 1)
             if v >= 2:
                 finish(v - 2)
+        reduce_nine(NV - 1)
         finish(NV - 2)
         finish(NV - 1)
 
@@ -269,16 +283,15 @@ def tile_involution2d_pa_kernel(tc, x, Wi, bi, w_span, out_0, out_1):
         fac = const.tile([P, 1], F32)
         nc.vector.tensor_scalar(out=fac[:], in0=rec[:], scalar1=448.0, scalar2=None, op0=ALU.mult)
 
-        flat = out_keep[:].rearrange("p v c -> p (v c)")
         for piece in range(4):
             f8 = fpool.tile([P, 2048], FP8, tag="f8", name="f8")
             for sub in range(4):
                 a = 512 * sub
                 b = 2048 * piece + a
                 if (4 * piece + sub) % 8 in S_SUBS:
-                    nc.scalar.activation(out=f8[:, a:a + 512], in_=flat[:, b:b + 512], func=ACT.Identity,
+                    nc.scalar.activation(out=f8[:, a:a + 512], in_=out_keep[:, b:b + 512], func=ACT.Identity,
                                          scale=fac[:, 0:1], bias=zcol[:, 0:1], saturate=False)
                 else:
-                    nc.vector.tensor_scalar(out=f8[:, a:a + 512], in0=flat[:, b:b + 512], scalar1=fac[:, 0:1],
+                    nc.vector.tensor_scalar(out=f8[:, a:a + 512], in0=out_keep[:, b:b + 512], scalar1=fac[:, 0:1],
                                             scalar2=None, op0=ALU.mult, saturate=False)
             nc.sync.dma_start(out=o1[:, 2048 * piece:2048 * (piece + 1)], in_=f8[:].bitcast(U8))

@@ -221,11 +221,10 @@ def tile_involution2d_pa_kernel(tc, x, Wi, bi, w_span, out_0, out_1):
 
             on_gpsimd(0, 5, rows[0][:, 0:5 * Q])
             on_gpsimd(11, 5, rows[2][:, 48:48 + 5 * Q])
-            on_gpsimd(6, 2, rows[1][:, 96:96 + 2 * Q])
             nc.vector.tensor_tensor(
-                out=prod[:, 8:10, :, :],
-                in0=rows[1][:, 96 + 2 * Q:96 + 4 * Q].rearrange("p (g j m) -> p g j m", j=16, m=9),
-                in1=wps[:, 27:45].rearrange("p (g m) -> p g m", m=9).unsqueeze(2).to_broadcast([P, 2, 16, 9]),
+                out=prod[:, 6:10, :, :],
+                in0=rows[1][:, 96:96 + 4 * Q].rearrange("p (g j m) -> p g j m", j=16, m=9),
+                in1=wps[:, 9:45].rearrange("p (g m) -> p g m", m=9).unsqueeze(2).to_broadcast([P, 4, 16, 9]),
                 op=ALU.mult,
             )
             nc.vector.tensor_tensor(

@@ -20,10 +20,12 @@ F = 256
 Q = 144
 FLOPS = 2 * 4096 * 1024 * 256 + 2 * 4096 * 2304
 
-XR = 12
+XR = 8
 BLK = 130
-R = 16
-CHUNKS = [(0, 2), (2, 2)] + [(v, 4) for v in range(4, NV, 4)]
+R = 12
+OFF = (48, 0, 0)
+XL = (R + 2) * F + 64
+CHUNKS = [(0, 1), (1, 1), (2, 2)] + [(v, 4) for v in range(4, NV, 4)]
 AHEAD = 8
 LOOK = 2
 S_SUBS = (2, 5, 7)
@@ -46,7 +48,7 @@ def tile_involution2d_pa_kernel(tc, x, Wi, bi, w_span, out_0, out_1):
         psx = ctx.enter_context(tc.psum_pool(name="psx", bufs=2))
         psa = ctx.enter_context(tc.psum_pool(name="psa", bufs=2))
         pst = ctx.enter_context(tc.psum_pool(name="pst", bufs=1))
-        psw = ctx.enter_context(tc.psum_pool(name="psw", bufs=2))
+        psw = ctx.enter_context(tc.psum_pool(name="psw", bufs=1))
 
         xtiles = {}
 
@@ -59,15 +61,15 @@ def tile_involution2d_pa_kernel(tc, x, Wi, bi, w_span, out_0, out_1):
         load_chunk(0)
         wi_raw = const.tile([P, 2, 4, F], BF16)
         nc.sync.dma_start(out=wi_raw[:], in_=Wi.rearrange("(g p j) c -> p g j c", g=2, j=4))
+        load_chunk(1)
         bias = []
         for h in range(2):
             b_h = const.tile([P, 1], BF16, name="bias%d" % h)
             nc.sync.dma_start(out=b_h[:], in_=bi[128 * h:128 * (h + 1)].rearrange("(p o) -> p o", o=1))
             bias.append(b_h)
-        load_chunk(1)
-        w_all = const.tile([P, NV * Q], BF16)
-        nc.sync.dma_start(out=w_all[:], in_=wv)
         load_chunk(2)
+        w_all = const.tile([P, NV, Q], BF16)
+        nc.sync.dma_start(out=w_all[:].rearrange("p v q -> p (v q)"), in_=wv)
 
         ident = const.tile([P, P], F32)
         make_identity(nc, ident[:])
@@ -80,10 +82,10 @@ def tile_involution2d_pa_kernel(tc, x, Wi, bi, w_span, out_0, out_1):
             t_h = const.tile([P, XR, BLK], F32, name="x_t%d" % h)
             nc.gpsimd.memset(t_h[:, :, 0:BLK:BLK - 1], 0.0)
             x_t.append(t_h)
-        xp = const.tile([P, 3, R + 2, F], F32)
-        nc.gpsimd.memset(xp[:, :, 0, :], 0.0)
+        xp = const.tile([P, 3, XL], F32)
+        nc.gpsimd.memset(xp[:, :, 0:F + 48], 0.0)
         out_keep = const.tile([P, NV * F], F32)
-        pm = const.tile([P, NV], F32)
+        pm = const.tile([P, NV // 2], F32)
         msum = const.tile([P, 2], F32)
         nc.vector.tensor_reduce(out=msum[:, 0:1], in_=ident[:, 0:P:32], axis=AX.X, op=ALU.add)
         nc.vector.tensor_reduce(out=msum[:, 1:2], in_=ident[:, 31:P:32], axis=AX.X, op=ALU.add)
@@ -99,6 +101,12 @@ def tile_involution2d_pa_kernel(tc, x, Wi, bi, w_span, out_0, out_1):
             scales=wi_scales[:],
             in_=wi_grp[:].rearrange("p g c j -> p (g c j)"),
         )
+
+        w_g = const.tile([P, NV, 90], BF16)
+        nc.gpsimd.tensor_scalar(out=w_g[:, :, 0:45], in0=w_all[:, :, 0:45], scalar1=1.0, scalar2=0.0,
+                                op0=ALU.mult, op1=ALU.add)
+        nc.gpsimd.tensor_scalar(out=w_g[:, :, 45:90], in0=w_all[:, :, 99:144], scalar1=1.0, scalar2=0.0,
+                                op0=ALU.mult, op1=ALU.add)
 
         grps = {}
 
@@ -174,63 +182,50 @@ def tile_involution2d_pa_kernel(tc, x, Wi, bi, w_span, out_0, out_1):
                         found.append(s)
             return found
 
-        def to_pixels(vp):
-            pta = pst.tile([P, 2, F], F32, tag="pta", name="pta")
-            ptb = pst.tile([P, F], F32, tag="ptb", name="ptb")
-            parts = [pta[:, 0, :], pta[:, 1, :], ptb[:]]
-            for i in range(3):
-                for h in range(2):
-                    nc.tensor.transpose(parts[i][:, h * P:(h + 1) * P], x_t[h][:, vp % XR, i:i + P], ident[:])
+        def block(i, s):
+            return xp[:, i, OFF[i] + F * s:OFF[i] + F * (s + 1)]
+
+        def to_pixels(vp, i):
+            pt = pst.tile([P, F], F32, tag="pt%d" % i, name="pt%d" % i)
+            for h in range(2):
+                nc.tensor.transpose(pt[:, h * P:(h + 1) * P], x_t[h][:, vp % XR, i:i + P], ident[:])
             for s in slots_of(vp + 1):
-                nc.scalar.activation(out=xp[:, 0, s, :], in_=parts[0], func=ACT.Copy, scale=mask[:, 0:1])
-                nc.scalar.copy(out=xp[:, 1, s, :], in_=parts[1])
-                nc.scalar.activation(out=xp[:, 2, s, :], in_=parts[2], func=ACT.Copy, scale=mask[:, 1:2])
+                if i == 1:
+                    nc.scalar.copy(out=block(1, s), in_=pt[:])
+                else:
+                    nc.scalar.activation(out=block(i, s), in_=pt[:], func=ACT.Copy, scale=mask[:, i // 2:i // 2 + 1])
 
         wtiles = {}
-        cuts = {}
+        mids = {}
         prods = {}
 
         def weights(v):
-            wps = psw.tile([P, 90], F32, tag="wps", name="wps")
-            nc.tensor.matmul(out=wps[:], lhsT=ident_bf[:], rhs=w_all[:, Q * v + 45:Q * v + 135], start=True, stop=True)
+            wps = psw.tile([P, 54], F32, tag="wps", name="wps")
+            nc.tensor.matmul(out=wps[:], lhsT=ident_bf[:], rhs=w_all[:, v, 45:99], start=True, stop=True)
             wtiles[v] = wps
 
-        def cut_groups(v):
-            base = v % R
-            cut = ppool.tile([P, 2, Q], F32, tag="cut", name="cut")
-            nc.scalar.copy(out=cut[:, 0, 0:48], in_=xp[:, 0, base + 2, 208:256])
-            nc.scalar.copy(out=cut[:, 0, 48:144], in_=xp[:, 1, base, 0:96])
-            nc.scalar.copy(out=cut[:, 1, 0:96], in_=xp[:, 1, base + 2, 160:256])
-            nc.scalar.copy(out=cut[:, 1, 96:144], in_=xp[:, 2, base, 0:48])
-            cuts[v] = cut
+        def middle(v):
+            b0 = F * (v % R)
+            mid = ppool.tile([P, 6 * Q], F32, tag="mid", name="mid")
+            nc.scalar.copy(out=mid[:, 0:48], in_=xp[:, 0, OFF[0] + b0 + 720:OFF[0] + b0 + 768])
+            nc.scalar.copy(out=mid[:, 48:816], in_=xp[:, 1, b0:b0 + 768])
+            nc.scalar.copy(out=mid[:, 816:864], in_=xp[:, 2, b0:b0 + 48])
+            mids[v] = mid
 
         def involve(v):
-            base = v % R
-            wps = wtiles[v]
-            prod = ppool.tile([P, 16, 16, 9], F32, tag="prod", name="prod")
-            rows = [xp[:, i, base:base + 3, :].rearrange("p s c -> p (s c)") for i in range(3)]
-
-            def on_gpsimd(g0, n, src):
-                nc.gpsimd.tensor_tensor(
-                    out=prod[:, g0:g0 + n, :, :],
-                    in0=src.rearrange("p (g j m) -> p g j m", j=16, m=9),
-                    in1=w_all[:, Q * v + 9 * g0:Q * v + 9 * (g0 + n)].rearrange("p (g m) -> p g m", m=9).unsqueeze(
-                        2).to_broadcast([P, n, 16, 9]),
-                    op=ALU.mult,
-                )
-
-            on_gpsimd(0, 5, rows[0][:, 0:5 * Q])
-            on_gpsimd(11, 5, rows[2][:, 48:48 + 5 * Q])
-            nc.vector.tensor_tensor(
-                out=prod[:, 6:10, :, :],
-                in0=rows[1][:, 96:96 + 4 * Q].rearrange("p (g j m) -> p g j m", j=16, m=9),
-                in1=wps[:, 9:45].rearrange("p (g m) -> p g m", m=9).unsqueeze(2).to_broadcast([P, 4, 16, 9]),
+            b0 = F * (v % R)
+            mid = mids[v]
+            prod = ppool.tile([P, 2, 11 * Q], F32, tag="prod", name="prod")
+            nc.gpsimd.tensor_tensor(
+                out=prod[:, :, 0:5 * Q],
+                in0=xp[:, 0:3:2, b0 + 48:b0 + 48 + 5 * Q],
+                in1=w_g[:, v, :].rearrange("p (g m) -> p g m", m=9).unsqueeze(2).to_broadcast([P, 10, 16, 9]),
                 op=ALU.mult,
             )
             nc.vector.tensor_tensor(
-                out=prod[:, 5:11:5, :, :],
-                in0=cuts[v][:].rearrange("p g (j m) -> p g j m", m=9),
-                in1=wps[:].rearrange("p (g r) -> p g r", r=45)[:, :, 0:9].unsqueeze(2).to_broadcast([P, 2, 16, 9]),
+                out=prod[:, 0, 5 * Q:11 * Q].rearrange("p (g j m) -> p g j m", j=16, m=9),
+                in0=mid[:].rearrange("p (g j m) -> p g j m", j=16, m=9),
+                in1=wtiles[v][:].rearrange("p (g m) -> p g m", m=9).unsqueeze(2).to_broadcast([P, 6, 16, 9]),
                 op=ALU.mult,
             )
             prods[v] = prod
@@ -238,38 +233,44 @@ def tile_involution2d_pa_kernel(tc, x, Wi, bi, w_span, out_0, out_1):
         def reduce_nine(v):
             nc.vector.tensor_reduce(
                 out=out_keep[:, F * v:F * (v + 1)],
-                in_=prods[v][:].rearrange("p g j m -> p (g j) m"),
+                in_=prods[v][:].rearrange("p a f -> p (a f)")[:, 0:16 * Q].rearrange("p (o m) -> p o m", m=9),
                 axis=AX.X,
                 op=ALU.add,
             )
 
         def finish(v):
-            nc.vector.tensor_reduce(out=pm[:, v:v + 1], in_=out_keep[:, F * v:F * (v + 1)], axis=AX.X, op=ALU.max,
-                                    apply_absolute_value=True)
-            nc.sync.dma_start(out=o0[:, v, :], in_=out_keep[:, F * v:F * (v + 1)])
+            nc.vector.tensor_reduce(out=pm[:, v // 2:v // 2 + 1], in_=out_keep[:, F * v:F * (v + 2)], axis=AX.X,
+                                    op=ALU.max, apply_absolute_value=True)
+            nc.sync.dma_start(out=o0[:, v:v + 2, :], in_=out_keep[:, F * v:F * (v + 2)].rearrange("p (v c) -> p v c", c=F))
 
-        advance(3)
-        for vp in range(LOOK + 1):
-            to_pixels(vp)
+        advance(1)
+        for vp, i in ((0, 0), (0, 2), (1, 0), (1, 2), (0, 1), (1, 1)):
+            to_pixels(vp, i)
         weights(0)
-        cut_groups(0)
+        middle(0)
+        advance(3)
+        for i in (0, 2, 1):
+            to_pixels(2, i)
         for v in range(NV):
             advance(v + AHEAD)
             if v + 1 + LOOK < NV:
-                to_pixels(v + 1 + LOOK)
+                for i in (0, 2, 1):
+                    to_pixels(v + 1 + LOOK, i)
             if v == NV - 4:
-                nc.gpsimd.memset(xp[:, :, R + 1, :], 0.0)
+                for s in slots_of(NV + 1):
+                    nc.gpsimd.memset(block(0, s), 0.0)
+                    nc.gpsimd.memset(xp[:, 1:3, F * s:F * (s + 1)], 0.0)
+            if v + 1 < NV:
+                middle(v + 1)
+            involve(v)
             if v + 1 < NV:
                 weights(v + 1)
-                cut_groups(v + 1)
-            involve(v)
             if v >= 1:
                 reduce_nine(v - 1)
-            if v >= 2:
-                finish(v - 2)
+            if v >= 3 and v % 2 == 1:
+                finish(v - 3)
         reduce_nine(NV - 1)
         finish(NV - 2)
-        finish(NV - 1)
 
         pmax = const.tile([P, 1], F32)
         nc.vector.tensor_reduce(out=pmax[:], in_=pm[:], axis=AX.X, op=ALU.max)

@@ -29,12 +29,13 @@ CHUNKS = [(0, 1), (1, 1), (2, 2)] + [(v, 4) for v in range(4, NV, 4)]
 AHEAD = 8
 LOOK = 2
 S_SUBS = (2, 5, 7)
+W_FIRST = 4
 
 
 def tile_involution2d_pa_kernel(tc, x, Wi, bi, w_span, out_0, out_1):
     nc = tc.nc
     xv = x.rearrange("b u v k -> (b u) v k")
-    wv = w_span.rearrange("b u v q -> (b u) (v q)")
+    wv = w_span.rearrange("b u v q -> (b u) v q")
     o0 = out_0.rearrange("b u v c -> (b u) v c")
     o1 = out_1.rearrange("b u v c -> (b u) (v c)")
 
@@ -44,7 +45,7 @@ def tile_involution2d_pa_kernel(tc, x, Wi, bi, w_span, out_0, out_1):
         gpool = ctx.enter_context(tc.tile_pool(name="gpool", bufs=2))
         cpool = ctx.enter_context(tc.tile_pool(name="cpool", bufs=2))
         ppool = ctx.enter_context(tc.tile_pool(name="ppool", bufs=3))
-        fpool = ctx.enter_context(tc.tile_pool(name="fpool", bufs=4))
+        fpool = ctx.enter_context(tc.tile_pool(name="fpool", bufs=8))
         psx = ctx.enter_context(tc.psum_pool(name="psx", bufs=2))
         psa = ctx.enter_context(tc.psum_pool(name="psa", bufs=2))
         pst = ctx.enter_context(tc.psum_pool(name="pst", bufs=1))
@@ -62,14 +63,15 @@ def tile_involution2d_pa_kernel(tc, x, Wi, bi, w_span, out_0, out_1):
         wi_raw = const.tile([P, 2, 4, F], BF16)
         nc.sync.dma_start(out=wi_raw[:], in_=Wi.rearrange("(g p j) c -> p g j c", g=2, j=4))
         load_chunk(1)
+        w_all = const.tile([P, NV, Q], BF16)
+        nc.sync.dma_start(out=w_all[:, 0:W_FIRST, :], in_=wv[:, 0:W_FIRST, :])
         bias = []
         for h in range(2):
             b_h = const.tile([P, 1], BF16, name="bias%d" % h)
             nc.sync.dma_start(out=b_h[:], in_=bi[128 * h:128 * (h + 1)].rearrange("(p o) -> p o", o=1))
             bias.append(b_h)
         load_chunk(2)
-        w_all = const.tile([P, NV, Q], BF16)
-        nc.sync.dma_start(out=w_all[:].rearrange("p v q -> p (v q)"), in_=wv)
+        nc.sync.dma_start(out=w_all[:, W_FIRST:NV, :], in_=wv[:, W_FIRST:NV, :])
 
         ident = const.tile([P, P], F32)
         make_identity(nc, ident[:])
@@ -85,7 +87,7 @@ def tile_involution2d_pa_kernel(tc, x, Wi, bi, w_span, out_0, out_1):
         xp = const.tile([P, 3, XL], F32)
         nc.gpsimd.memset(xp[:, :, 0:F + 48], 0.0)
         out_keep = const.tile([P, NV * F], F32)
-        pm = const.tile([P, NV // 2], F32)
+        pm = const.tile([P, NV // 4 + 1], F32)
         msum = const.tile([P, 2], F32)
         nc.vector.tensor_reduce(out=msum[:, 0:1], in_=ident[:, 0:P:32], axis=AX.X, op=ALU.add)
         nc.vector.tensor_reduce(out=msum[:, 1:2], in_=ident[:, 31:P:32], axis=AX.X, op=ALU.add)
@@ -103,9 +105,9 @@ def tile_involution2d_pa_kernel(tc, x, Wi, bi, w_span, out_0, out_1):
         )
 
         w_g = const.tile([P, NV, 90], BF16)
-        nc.gpsimd.tensor_scalar(out=w_g[:, :, 0:45], in0=w_all[:, :, 0:45], scalar1=1.0, scalar2=0.0,
+        nc.gpsimd.tensor_scalar(out=w_g[:, 0:W_FIRST, 0:45], in0=w_all[:, 0:W_FIRST, 0:45], scalar1=1.0, scalar2=0.0,
                                 op0=ALU.mult, op1=ALU.add)
-        nc.gpsimd.tensor_scalar(out=w_g[:, :, 45:90], in0=w_all[:, :, 99:144], scalar1=1.0, scalar2=0.0,
+        nc.gpsimd.tensor_scalar(out=w_g[:, 0:W_FIRST, 45:90], in0=w_all[:, 0:W_FIRST, 99:144], scalar1=1.0, scalar2=0.0,
                                 op0=ALU.mult, op1=ALU.add)
 
         grps = {}
@@ -198,6 +200,7 @@ def tile_involution2d_pa_kernel(tc, x, Wi, bi, w_span, out_0, out_1):
         wtiles = {}
         mids = {}
         prods = {}
+        finished = []
 
         def weights(v):
             wps = psw.tile([P, 54], F32, tag="wps", name="wps")
@@ -238,10 +241,12 @@ def tile_involution2d_pa_kernel(tc, x, Wi, bi, w_span, out_0, out_1):
                 op=ALU.add,
             )
 
-        def finish(v):
-            nc.vector.tensor_reduce(out=pm[:, v // 2:v // 2 + 1], in_=out_keep[:, F * v:F * (v + 2)], axis=AX.X,
+        def finish(v, n):
+            col = len(finished)
+            finished.append(v)
+            nc.vector.tensor_reduce(out=pm[:, col:col + 1], in_=out_keep[:, F * v:F * (v + n)], axis=AX.X,
                                     op=ALU.max, apply_absolute_value=True)
-            nc.sync.dma_start(out=o0[:, v:v + 2, :], in_=out_keep[:, F * v:F * (v + 2)].rearrange("p (v c) -> p v c", c=F))
+            nc.sync.dma_start(out=o0[:, v:v + n, :], in_=out_keep[:, F * v:F * (v + n)].rearrange("p (v c) -> p v c", c=F))
 
         advance(1)
         for vp, i in ((0, 0), (0, 2), (1, 0), (1, 2), (0, 1), (1, 1)):
@@ -263,14 +268,19 @@ def tile_involution2d_pa_kernel(tc, x, Wi, bi, w_span, out_0, out_1):
             if v + 1 < NV:
                 middle(v + 1)
             involve(v)
+            if v % W_FIRST == 0 and v + W_FIRST < NV:
+                nxt = slice(v + W_FIRST, v + 2 * W_FIRST)
+                nc.scalar.copy(out=w_g[:, nxt, 0:45], in_=w_all[:, nxt, 0:45])
+                nc.scalar.copy(out=w_g[:, nxt, 45:90], in_=w_all[:, nxt, 99:144])
             if v + 1 < NV:
                 weights(v + 1)
             if v >= 1:
                 reduce_nine(v - 1)
-            if v >= 3 and v % 2 == 1:
-                finish(v - 3)
+            if v >= 5 and v % 4 == 1:
+                finish(v - 5, 4)
+        finish(NV - 4, 2)
         reduce_nine(NV - 1)
-        finish(NV - 2)
+        finish(NV - 2, 2)
 
         pmax = const.tile([P, 1], F32)
         nc.vector.tensor_reduce(out=pmax[:], in_=pm[:], axis=AX.X, op=ALU.max)
@@ -283,15 +293,15 @@ def tile_involution2d_pa_kernel(tc, x, Wi, bi, w_span, out_0, out_1):
         fac = const.tile([P, 1], F32)
         nc.vector.tensor_scalar(out=fac[:], in0=rec[:], scalar1=448.0, scalar2=None, op0=ALU.mult)
 
-        for piece in range(4):
-            f8 = fpool.tile([P, 2048], FP8, tag="f8", name="f8")
-            for sub in range(4):
+        for piece in range(8):
+            f8 = fpool.tile([P, 1024], FP8, tag="f8", name="f8")
+            for sub in range(2):
                 a = 512 * sub
-                b = 2048 * piece + a
-                if (4 * piece + sub) % 8 in S_SUBS:
+                b = 1024 * piece + a
+                if (2 * piece + sub) % 8 in S_SUBS:
                     nc.scalar.activation(out=f8[:, a:a + 512], in_=out_keep[:, b:b + 512], func=ACT.Identity,
                                          scale=fac[:, 0:1], bias=zcol[:, 0:1], saturate=False)
                 else:
                     nc.vector.tensor_scalar(out=f8[:, a:a + 512], in0=out_keep[:, b:b + 512], scalar1=fac[:, 0:1],
                                             scalar2=None, op0=ALU.mult, saturate=False)
-            nc.sync.dma_start(out=o1[:, 2048 * piece:2048 * (piece + 1)], in_=f8[:].bitcast(U8))
+            nc.sync.dma_start(out=o1[:, 1024 * piece:1024 * (piece + 1)], in_=f8[:].bitcast(U8))

@@ -18,16 +18,19 @@ NV = 32
 C = 1024
 F = 256
 Q = 144
+FLAT = 9 * F
 FLOPS = 2 * 4096 * 1024 * 256 + 2 * 4096 * 2304
 
 XR = 8
 BLK = 130
 R = 12
-OFF = (48, 0, 0)
-XL = (R + 2) * F + 64
+XL = (R + 2) * F
 CHUNKS = [(0, 1), (1, 1), (2, 2)] + [(v, 4) for v in range(4, NV, 4)]
 AHEAD = 8
 LOOK = 2
+LAG = 2
+NVC = 12
+V_COLS = [(k * (NV - 1) + (NVC - 1) // 2) // (NVC - 1) for k in range(NVC)]
 S_SUBS = (2, 5, 7)
 W_FIRST = 4
 
@@ -44,7 +47,7 @@ def tile_involution2d_pa_kernel(tc, x, Wi, bi, w_span, out_0, out_1):
         xpool = ctx.enter_context(tc.tile_pool(name="xpool", bufs=3))
         gpool = ctx.enter_context(tc.tile_pool(name="gpool", bufs=2))
         cpool = ctx.enter_context(tc.tile_pool(name="cpool", bufs=2))
-        ppool = ctx.enter_context(tc.tile_pool(name="ppool", bufs=3))
+        ppool = ctx.enter_context(tc.tile_pool(name="ppool", bufs=5))
         fpool = ctx.enter_context(tc.tile_pool(name="fpool", bufs=8))
         psx = ctx.enter_context(tc.psum_pool(name="psx", bufs=2))
         psa = ctx.enter_context(tc.psum_pool(name="psa", bufs=2))
@@ -85,7 +88,9 @@ def tile_involution2d_pa_kernel(tc, x, Wi, bi, w_span, out_0, out_1):
             nc.gpsimd.memset(t_h[:, :, 0:BLK:BLK - 1], 0.0)
             x_t.append(t_h)
         xp = const.tile([P, 3, XL], F32)
-        nc.gpsimd.memset(xp[:, :, 0:F + 48], 0.0)
+        nc.gpsimd.memset(xp[:, :, 0:F], 0.0)
+        zblk = const.tile([P, F], F32)
+        nc.gpsimd.memset(zblk[:], 0.0)
         out_keep = const.tile([P, NV * F], F32)
         pm = const.tile([P, NV // 4 + 1], F32)
         msum = const.tile([P, 2], F32)
@@ -103,12 +108,6 @@ def tile_involution2d_pa_kernel(tc, x, Wi, bi, w_span, out_0, out_1):
             scales=wi_scales[:],
             in_=wi_grp[:].rearrange("p g c j -> p (g c j)"),
         )
-
-        w_g = const.tile([P, NV, 90], BF16)
-        nc.gpsimd.tensor_scalar(out=w_g[:, 0:W_FIRST, 0:45], in0=w_all[:, 0:W_FIRST, 0:45], scalar1=1.0, scalar2=0.0,
-                                op0=ALU.mult, op1=ALU.add)
-        nc.gpsimd.tensor_scalar(out=w_g[:, 0:W_FIRST, 45:90], in0=w_all[:, 0:W_FIRST, 99:144], scalar1=1.0, scalar2=0.0,
-                                op0=ALU.mult, op1=ALU.add)
 
         grps = {}
 
@@ -185,7 +184,7 @@ def tile_involution2d_pa_kernel(tc, x, Wi, bi, w_span, out_0, out_1):
             return found
 
         def block(i, s):
-            return xp[:, i, OFF[i] + F * s:OFF[i] + F * (s + 1)]
+            return xp[:, i, F * s:F * (s + 1)]
 
         def to_pixels(vp, i):
             pt = pst.tile([P, F], F32, tag="pt%d" % i, name="pt%d" % i)
@@ -198,45 +197,37 @@ def tile_involution2d_pa_kernel(tc, x, Wi, bi, w_span, out_0, out_1):
                     nc.scalar.activation(out=block(i, s), in_=pt[:], func=ACT.Copy, scale=mask[:, i // 2:i // 2 + 1])
 
         wtiles = {}
-        mids = {}
         prods = {}
         finished = []
 
         def weights(v):
-            wps = psw.tile([P, 54], F32, tag="wps", name="wps")
-            nc.tensor.matmul(out=wps[:], lhsT=ident_bf[:], rhs=w_all[:, v, 45:99], start=True, stop=True)
+            wps = psw.tile([P, Q], F32, tag="wps", name="wps")
+            nc.tensor.matmul(out=wps[:], lhsT=ident_bf[:], rhs=w_all[:, v, :], start=True, stop=True)
             wtiles[v] = wps
-
-        def middle(v):
-            b0 = F * (v % R)
-            mid = ppool.tile([P, 6 * Q], F32, tag="mid", name="mid")
-            nc.scalar.copy(out=mid[:, 0:48], in_=xp[:, 0, OFF[0] + b0 + 720:OFF[0] + b0 + 768])
-            nc.scalar.copy(out=mid[:, 48:816], in_=xp[:, 1, b0:b0 + 768])
-            nc.scalar.copy(out=mid[:, 816:864], in_=xp[:, 2, b0:b0 + 48])
-            mids[v] = mid
 
         def involve(v):
             b0 = F * (v % R)
-            mid = mids[v]
-            prod = ppool.tile([P, 2, 11 * Q], F32, tag="prod", name="prod")
-            nc.gpsimd.tensor_tensor(
-                out=prod[:, :, 0:5 * Q],
-                in0=xp[:, 0:3:2, b0 + 48:b0 + 48 + 5 * Q],
-                in1=w_g[:, v, :].rearrange("p (g m) -> p g m", m=9).unsqueeze(2).to_broadcast([P, 10, 16, 9]),
-                op=ALU.mult,
-            )
-            nc.vector.tensor_tensor(
-                out=prod[:, 0, 5 * Q:11 * Q].rearrange("p (g j m) -> p g j m", j=16, m=9),
-                in0=mid[:].rearrange("p (g j m) -> p g j m", j=16, m=9),
-                in1=wtiles[v][:].rearrange("p (g m) -> p g m", m=9).unsqueeze(2).to_broadcast([P, 6, 16, 9]),
-                op=ALU.mult,
-            )
+            prod = ppool.tile([P, FLAT], F32, tag="prod", name="prod")
+            if v in V_COLS:
+                nc.vector.tensor_tensor(
+                    out=prod[:].rearrange("p (a f) -> p a f", a=3),
+                    in0=xp[:, :, b0:b0 + 3 * F],
+                    in1=wtiles[v][:].rearrange("p (g m) -> p g m", m=9).unsqueeze(2).to_broadcast([P, 16, 16, 9]),
+                    op=ALU.mult,
+                )
+            else:
+                nc.gpsimd.tensor_tensor(
+                    out=prod[:].rearrange("p (a f) -> p a f", a=3),
+                    in0=xp[:, :, b0:b0 + 3 * F],
+                    in1=w_all[:, v, :].rearrange("p (g m) -> p g m", m=9).unsqueeze(2).to_broadcast([P, 16, 16, 9]),
+                    op=ALU.mult,
+                )
             prods[v] = prod
 
         def reduce_nine(v):
             nc.vector.tensor_reduce(
                 out=out_keep[:, F * v:F * (v + 1)],
-                in_=prods[v][:].rearrange("p a f -> p (a f)")[:, 0:16 * Q].rearrange("p (o m) -> p o m", m=9),
+                in_=prods[v][:].rearrange("p (o m) -> p o m", m=9),
                 axis=AX.X,
                 op=ALU.add,
             )
@@ -249,37 +240,31 @@ def tile_involution2d_pa_kernel(tc, x, Wi, bi, w_span, out_0, out_1):
             nc.sync.dma_start(out=o0[:, v:v + n, :], in_=out_keep[:, F * v:F * (v + n)].rearrange("p (v c) -> p v c", c=F))
 
         advance(1)
-        for vp, i in ((0, 0), (0, 2), (1, 0), (1, 2), (0, 1), (1, 1)):
+        for vp, i in ((0, 0), (0, 1), (0, 2), (1, 0), (1, 1), (1, 2)):
             to_pixels(vp, i)
-        weights(0)
-        middle(0)
+        weights(V_COLS[0])
         advance(3)
-        for i in (0, 2, 1):
+        for i in (0, 1, 2):
             to_pixels(2, i)
-        for v in range(NV):
-            advance(v + AHEAD)
-            if v + 1 + LOOK < NV:
-                for i in (0, 2, 1):
-                    to_pixels(v + 1 + LOOK, i)
-            if v == NV - 4:
-                for s in slots_of(NV + 1):
-                    nc.gpsimd.memset(block(0, s), 0.0)
-                    nc.gpsimd.memset(xp[:, 1:3, F * s:F * (s + 1)], 0.0)
-            if v + 1 < NV:
-                middle(v + 1)
-            involve(v)
-            if v % W_FIRST == 0 and v + W_FIRST < NV:
-                nxt = slice(v + W_FIRST, v + 2 * W_FIRST)
-                nc.scalar.copy(out=w_g[:, nxt, 0:45], in_=w_all[:, nxt, 0:45])
-                nc.scalar.copy(out=w_g[:, nxt, 45:90], in_=w_all[:, nxt, 99:144])
-            if v + 1 < NV:
-                weights(v + 1)
-            if v >= 1:
-                reduce_nine(v - 1)
-            if v >= 5 and v % 4 == 1:
-                finish(v - 5, 4)
-        finish(NV - 4, 2)
-        reduce_nine(NV - 1)
+        for v in range(NV + LAG):
+            if v < NV:
+                advance(v + AHEAD)
+                if v + 1 + LOOK < NV:
+                    for i in (0, 1, 2):
+                        to_pixels(v + 1 + LOOK, i)
+                if v == NV - 4:
+                    for s in slots_of(NV + 1):
+                        nc.scalar.copy(out=xp[:, :, F * s:F * (s + 1)], in_=zblk[:].unsqueeze(1).to_broadcast([P, 3, F]))
+                involve(v)
+                if v in V_COLS and V_COLS.index(v) + 1 < NVC:
+                    weights(V_COLS[V_COLS.index(v) + 1])
+            c = v - LAG
+            if c >= 0:
+                reduce_nine(c)
+                if c % 4 == 0 and c >= 4:
+                    finish(c - 4, 4)
+                if c == NV - 2:
+                    finish(NV - 4, 2)
         finish(NV - 2, 2)
 
         pmax = const.tile([P, 1], F32)

@@ -21,12 +21,11 @@ Q = 144
 FLAT = 9 * F
 FLOPS = 2 * 4096 * 1024 * 256 + 2 * 4096 * 2304
 
-XR = 8
+XR = 16
 BLK = 130
 R = 12
 XL = (R + 2) * F
 CHUNKS = [(0, 1), (1, 1), (2, 2)] + [(v, 4) for v in range(4, NV, 4)]
-AHEAD = 8
 LOOK = 2
 LAG = 2
 NVC = 12
@@ -155,17 +154,26 @@ def tile_involution2d_pa_kernel(tc, x, Wi, bi, w_span, out_0, out_1):
                                      func=ACT.Identity, bias=bias[h][:, 0:1])
 
         steps = []
-        last_step = {}
-        for k, chunk in enumerate(CHUNKS):
-            for r in range(chunk[1]):
-                steps.append((0, k, r))
-                last_step[chunk[0] + r] = len(steps)
+        for k in range(4):
+            steps.extend([(0, k, r) for r in range(CHUNKS[k][1])])
             steps.append((1, k, 0))
-            last_step[chunk[0] + chunk[1] - 1] = len(steps)
+        for k in range(4, len(CHUNKS), 2):
+            for kk in (k, k + 1):
+                steps.extend([(0, kk, r) for r in range(CHUNKS[kk][1])])
+            steps.append((1, k, 0))
+            steps.append((1, k + 1, 0))
+        turned = {}
+        projected = {}
+        for n, step in enumerate(steps):
+            v0, nv = CHUNKS[step[1]]
+            if step[0] == 0:
+                turned[v0 + step[2]] = n + 1
+            else:
+                for r in range(nv):
+                    projected[v0 + r] = n + 1
         done = [0]
 
-        def advance(v):
-            goal = last_step[min(v, NV - 1)]
+        def run_to(goal):
             while done[0] < goal:
                 kind, k, r = steps[done[0]]
                 if kind == 0:
@@ -239,16 +247,23 @@ def tile_involution2d_pa_kernel(tc, x, Wi, bi, w_span, out_0, out_1):
                                     op=ALU.max, apply_absolute_value=True)
             nc.sync.dma_start(out=o0[:, v:v + n, :], in_=out_keep[:, F * v:F * (v + n)].rearrange("p (v c) -> p v c", c=F))
 
-        advance(1)
+        run_to(projected[1])
         for vp, i in ((0, 0), (0, 1), (0, 2), (1, 0), (1, 1), (1, 2)):
             to_pixels(vp, i)
         weights(V_COLS[0])
-        advance(3)
+        run_to(projected[3])
         for i in (0, 1, 2):
             to_pixels(2, i)
         for v in range(NV + LAG):
             if v < NV:
-                advance(v + AHEAD)
+                if v < 4:
+                    run_to(turned[9 + 2 * v])
+                    if v == 3:
+                        run_to(projected[15])
+                elif v + 12 < NV:
+                    run_to(turned[v + 12])
+                    if v % 8 == 3:
+                        run_to(projected[v + 12])
                 if v + 1 + LOOK < NV:
                     for i in (0, 1, 2):
                         to_pixels(v + 1 + LOOK, i)

@@ -31,6 +31,7 @@ LAG = 2
 NVC = 12
 V_COLS = [(k * (NV - 1) + (NVC - 1) // 2) // (NVC - 1) for k in range(NVC)]
 S_SUBS = (2, 5, 7)
+MEETS = {3: (15, 2, 4), 12: (23, 12, 13), 20: (31, 19, 21)}
 W_FIRST = 4
 
 
@@ -46,12 +47,13 @@ def tile_involution2d_pa_kernel(tc, x, Wi, bi, w_span, out_0, out_1):
         xpool = ctx.enter_context(tc.tile_pool(name="xpool", bufs=3))
         gpool = ctx.enter_context(tc.tile_pool(name="gpool", bufs=2))
         cpool = ctx.enter_context(tc.tile_pool(name="cpool", bufs=2))
-        ppool = ctx.enter_context(tc.tile_pool(name="ppool", bufs=5))
+        ppool = ctx.enter_context(tc.tile_pool(name="ppool", bufs=6))
         fpool = ctx.enter_context(tc.tile_pool(name="fpool", bufs=8))
         psx = ctx.enter_context(tc.psum_pool(name="psx", bufs=2))
         psa = ctx.enter_context(tc.psum_pool(name="psa", bufs=2))
         pst = ctx.enter_context(tc.psum_pool(name="pst", bufs=1))
         psw = ctx.enter_context(tc.psum_pool(name="psw", bufs=1))
+        ctx.enter_context(tc.manual_schedule(engines={mybir.EngineType.DVE}))
 
         xtiles = {}
 
@@ -205,6 +207,17 @@ def tile_involution2d_pa_kernel(tc, x, Wi, bi, w_span, out_0, out_1):
                     nc.scalar.activation(out=block(i, s), in_=pt[:], func=ACT.Copy, scale=mask[:, i // 2:i // 2 + 1])
 
         wtiles = {}
+        gated = {}
+        junk = const.tile([P, 8], F32)
+
+        def meet(chunks, last_col, next_col):
+            n_meet = len(gated)
+            nc.vector.tensor_copy(out=junk[:, 2 * n_meet:2 * n_meet + 2], in_=prods[last_col][:, 0:2])
+            run_to(projected[chunks])
+            w_gate = const.tile([P, Q], BF16, name="w_gate%d" % next_col)
+            nc.vector.tensor_copy(out=w_gate[:], in_=w_all[:, next_col, :])
+            gated[next_col] = w_gate[:]
+
         prods = {}
         finished = []
 
@@ -227,7 +240,7 @@ def tile_involution2d_pa_kernel(tc, x, Wi, bi, w_span, out_0, out_1):
                 nc.gpsimd.tensor_tensor(
                     out=prod[:].rearrange("p (a f) -> p a f", a=3),
                     in0=xp[:, :, b0:b0 + 3 * F],
-                    in1=w_all[:, v, :].rearrange("p (g m) -> p g m", m=9).unsqueeze(2).to_broadcast([P, 16, 16, 9]),
+                    in1=gated.get(v, w_all[:, v, :]).rearrange("p (g m) -> p g m", m=9).unsqueeze(2).to_broadcast([P, 16, 16, 9]),
                     op=ALU.mult,
                 )
             prods[v] = prod
@@ -254,32 +267,43 @@ def tile_involution2d_pa_kernel(tc, x, Wi, bi, w_span, out_0, out_1):
         run_to(projected[3])
         for i in (0, 1, 2):
             to_pixels(2, i)
+
+        def summed(c):
+            reduce_nine(c)
+            if c % 4 == 0 and c >= 4:
+                finish(c - 4, 4)
+            if c == NV - 2:
+                finish(NV - 4, 2)
+
         for v in range(NV + LAG):
-            if v < NV:
-                if v < 4:
-                    run_to(turned[9 + 2 * v])
-                    if v == 3:
-                        run_to(projected[15])
-                elif v + 12 < NV:
-                    run_to(turned[v + 12])
-                    if v % 8 == 3:
-                        run_to(projected[v + 12])
-                if v + 1 + LOOK < NV:
-                    for i in (0, 1, 2):
-                        to_pixels(v + 1 + LOOK, i)
-                if v == NV - 4:
-                    for s in slots_of(NV + 1):
-                        nc.scalar.copy(out=xp[:, :, F * s:F * (s + 1)], in_=zblk[:].unsqueeze(1).to_broadcast([P, 3, F]))
+            if v == 0:
+                run_to(turned[7])
+            elif v < 4:
+                run_to(turned[9 + 2 * v])
+            elif v + 12 < NV and v != 12:
+                run_to(turned[v + 12])
+            if v > 0 and v + 1 + LOOK < NV:
+                for i in (0, 1, 2):
+                    to_pixels(v + 1 + LOOK, i)
+            if v == NV - 4:
+                for s in slots_of(NV + 1):
+                    nc.scalar.copy(out=xp[:, :, F * s:F * (s + 1)], in_=zblk[:].unsqueeze(1).to_broadcast([P, 3, F]))
+            if v >= LAG and v - LAG > 0:
+                summed(v - LAG)
+            if v < NV and v in V_COLS:
                 involve(v)
-                if v in V_COLS and V_COLS.index(v) + 1 < NVC:
+                if V_COLS.index(v) + 1 < NVC:
                     weights(V_COLS[V_COLS.index(v) + 1])
-            c = v - LAG
-            if c >= 0:
-                reduce_nine(c)
-                if c % 4 == 0 and c >= 4:
-                    finish(c - 4, 4)
-                if c == NV - 2:
-                    finish(NV - 4, 2)
+            if v in MEETS:
+                meet(*MEETS[v])
+            if v + 1 < NV and v + 1 not in V_COLS:
+                involve(v + 1)
+            if v == 0:
+                for i in (0, 1, 2):
+                    to_pixels(1 + LOOK, i)
+                summed(0)
+                run_to(projected[7])
+                run_to(turned[9])
         finish(NV - 2, 2)
 
         pmax = const.tile([P, 1], F32)

@@ -92,8 +92,8 @@ def tile_involution2d_pa_kernel(tc, x, Wi, bi, w_span, out_0, out_1):
         nc.gpsimd.memset(xp[:, :, 0:F], 0.0)
         zblk = const.tile([P, F], F32)
         nc.gpsimd.memset(zblk[:], 0.0)
-        out_keep = const.tile([P, NV * F], F32)
-        pm = const.tile([P, NV // 4 + 1], F32)
+        out_keep = const.tile([P, NV * F + NV // 4], F32)
+        pm = out_keep[:, NV * F:NV * F + NV // 4]
         msum = const.tile([P, 2], F32)
         nc.vector.tensor_reduce(out=msum[:, 0:1], in_=ident[:, 0:P:32], axis=AX.X, op=ALU.add)
         nc.vector.tensor_reduce(out=msum[:, 1:2], in_=ident[:, 31:P:32], axis=AX.X, op=ALU.add)
@@ -273,7 +273,7 @@ def tile_involution2d_pa_kernel(tc, x, Wi, bi, w_span, out_0, out_1):
             if c % 4 == 0 and c >= 4:
                 finish(c - 4, 4)
             if c == NV - 2:
-                finish(NV - 4, 2)
+                finish(NV - 4, 3)
 
         for v in range(NV + LAG):
             if v == 0:
@@ -304,18 +304,19 @@ def tile_involution2d_pa_kernel(tc, x, Wi, bi, w_span, out_0, out_1):
                 summed(0)
                 run_to(projected[7])
                 run_to(turned[9])
-        finish(NV - 2, 2)
 
+        nc.sync.dma_start(out=o0[:, NV - 1, :], in_=out_keep[:, F * (NV - 1):F * NV])
         pmax = const.tile([P, 1], F32)
-        nc.vector.tensor_reduce(out=pmax[:], in_=pm[:], axis=AX.X, op=ALU.max)
+        nc.vector.tensor_reduce(out=pmax[:], in_=out_keep[:, F * (NV - 1):NV * F + NV // 4], axis=AX.X,
+                                op=ALU.max, apply_absolute_value=True)
         spread = psx.tile([P, P], F32, tag="xt", name="spread")
         nc.tensor.transpose(spread[:], pmax[:, 0:1].to_broadcast([P, P]), ident[:])
-        amax = const.tile([P, 1], F32)
-        nc.vector.tensor_reduce(out=amax[:], in_=spread[:], axis=AX.X, op=ALU.max)
-        rec = const.tile([P, 1], F32)
-        nc.vector.reciprocal(out=rec[:], in_=amax[:])
+        scaled = const.tile([P, P], F32)
+        step_size = const.tile([P, 1], F32)
+        nc.vector.tensor_scalar(out=scaled[:], in0=spread[:], scalar1=1.0 / 448.0, scalar2=None, op0=ALU.mult, op1=ALU.max,
+                                accum_out=step_size[:])
         fac = const.tile([P, 1], F32)
-        nc.vector.tensor_scalar(out=fac[:], in0=rec[:], scalar1=448.0, scalar2=None, op0=ALU.mult)
+        nc.vector.reciprocal(out=fac[:], in_=step_size[:])
 
         for piece in range(8):
             f8 = fpool.tile([P, 1024], FP8, tag="f8", name="f8")

@@ -31,6 +31,7 @@ LAG = 2
 NVC = 12
 V_COLS = [(k * (NV - 1) + (NVC - 1) // 2) // (NVC - 1) for k in range(NVC)]
 S_SUBS = (2, 5, 7)
+N_WARM = 9
 MEETS = {3: (15, 2, 4), 12: (23, 12, 13), 20: (31, 19, 21)}
 W_FIRST = 4
 
@@ -55,6 +56,18 @@ def tile_involution2d_pa_kernel(tc, x, Wi, bi, w_span, out_0, out_1):
         psw = ctx.enter_context(tc.psum_pool(name="psw", bufs=1))
         ctx.enter_context(tc.manual_schedule(engines={mybir.EngineType.DVE}))
 
+        zeros_bf = const.tile([P, 512], BF16)
+        nc.vector.memset(zeros_bf[:], 0.0)
+        warm = psw.tile([P, 512], F32, tag="wps", name="warm")
+        warmed = [0]
+
+        def keep_warm(n):
+            for i in range(n):
+                nc.tensor.matmul(out=warm[:], lhsT=zeros_bf[:, 0:P], rhs=zeros_bf[:], start=(warmed[0] == 0),
+                                 stop=(warmed[0] == N_WARM - 1))
+                warmed[0] += 1
+
+        keep_warm(4)
         xtiles = {}
 
         def load_chunk(k):
@@ -82,7 +95,6 @@ def tile_involution2d_pa_kernel(tc, x, Wi, bi, w_span, out_0, out_1):
         ident_bf = const.tile([P, P], BF16)
         make_identity(nc, ident_bf[:])
         zcol = const.tile([P, 1], F32)
-        nc.gpsimd.memset(zcol[:], 0.0)
         x_t = []
         for h in range(2):
             t_h = const.tile([P, XR, BLK], F32, name="x_t%d" % h)
@@ -260,8 +272,19 @@ def tile_involution2d_pa_kernel(tc, x, Wi, bi, w_span, out_0, out_1):
                                     op=ALU.max, apply_absolute_value=True)
             nc.sync.dma_start(out=o0[:, v:v + n, :], in_=out_keep[:, F * v:F * (v + n)].rearrange("p (v c) -> p v c", c=F))
 
+        run_to(turned[0])
+        keep_warm(1)
+        run_to(projected[0])
+        keep_warm(1)
+        run_to(turned[1])
+        keep_warm(1)
         run_to(projected[1])
-        for vp, i in ((0, 0), (0, 1), (0, 2), (1, 0), (1, 1), (1, 2)):
+        keep_warm(1)
+        for vp, i in ((0, 0), (0, 1), (0, 2)):
+            to_pixels(vp, i)
+        keep_warm(1)
+        nc.scalar.copy(out=zcol[:], in_=warm[:, 0:1])
+        for vp, i in ((1, 0), (1, 1), (1, 2)):
             to_pixels(vp, i)
         weights(V_COLS[0])
         run_to(projected[3])

from contextlib import ExitStack

import concourse.mybir as mybir
from concourse.masks import make_identity

F32 = mybir.dt.float32
BF16 = mybir.dt.bfloat16
U32 = mybir.dt.uint32
U8 = mybir.dt.uint8
FP8X4 = mybir.dt.float8_e4m3fn_x4
FP8 = mybir.dt.float8_e4m3fn
ALU = mybir.AluOpType
ACT = mybir.ActivationFunctionType
AX = mybir.AxisListType

P = 128
NV = 32
C = 1024
F = 256
Q = 144
FLAT = 9 * F
FLOPS = 2 * 4096 * 1024 * 256 + 2 * 4096 * 2304

XR = 16
BLK = 130
R = 12
XL = (R + 2) * F
CHUNKS = [(0, 1), (1, 1), (2, 2)] + [(v, 4) for v in range(4, NV, 4)]
LOOK = 2
LAG = 2
NVC = 12
V_COLS = [(k * (NV - 1) + (NVC - 1) // 2) // (NVC - 1) for k in range(NVC)]
S_SUBS = (2, 5, 7)
N_WARM = 9
MEETS = {3: (15, 2, 4), 12: (23, 12, 13), 20: (31, 19, 21)}
W_FIRST = 4


def tile_involution2d_pa_kernel(tc, x, Wi, bi, w_span, out_0, out_1):
    nc = tc.nc
    xv = x.rearrange("b u v k -> (b u) v k")
    wv = w_span.rearrange("b u v q -> (b u) v q")
    o0 = out_0.rearrange("b u v c -> (b u) v c")
    o1 = out_1.rearrange("b u v c -> (b u) (v c)")

    with ExitStack() as ctx:
        const = ctx.enter_context(tc.tile_pool(name="const", bufs=1))
        xpool = ctx.enter_context(tc.tile_pool(name="xpool", bufs=3))
        gpool = ctx.enter_context(tc.tile_pool(name="gpool", bufs=2))
        cpool = ctx.enter_context(tc.tile_pool(name="cpool", bufs=2))
        ppool = ctx.enter_context(tc.tile_pool(name="ppool", bufs=6))
        fpool = ctx.enter_context(tc.tile_pool(name="fpool", bufs=8))
        psx = ctx.enter_context(tc.psum_pool(name="psx", bufs=2))
        psa = ctx.enter_context(tc.psum_pool(name="psa", bufs=2))
        pst = ctx.enter_context(tc.psum_pool(name="pst", bufs=1))
        psw = ctx.enter_context(tc.psum_pool(name="psw", bufs=1))
        ctx.enter_context(tc.manual_schedule(engines={mybir.EngineType.DVE}))

        zeros_bf = const.tile([P, 512], BF16)
        nc.vector.memset(zeros_bf[:], 0.0)
        warm = psw.tile([P, 512], F32, tag="wps", name="warm")
        warmed = [0]

        def keep_warm(n):
            for i in range(n):
                nc.tensor.matmul(out=warm[:], lhsT=zeros_bf[:, 0:P], rhs=zeros_bf[:], start=(warmed[0] == 0),
                                 stop=(warmed[0] == N_WARM - 1))
                warmed[0] += 1

        keep_warm(4)
        xtiles = {}

        def load_chunk(k):
            v0, nv = CHUNKS[k]
            x_sb = xpool.tile([P, nv, C], BF16, tag="x", name="x_sb")
            nc.sync.dma_start(out=x_sb[:], in_=xv[:, v0:v0 + nv, :])
            xtiles[k] = x_sb

        load_chunk(0)
        wi_raw = const.tile([P, 2, 4, F], BF16)
        nc.sync.dma_start(out=wi_raw[:], in_=Wi.rearrange("(g p j) c -> p g j c", g=2, j=4))
        load_chunk(1)
        w_all = const.tile([P, NV, Q], BF16)
        nc.sync.dma_start(out=w_all[:, 0:W_FIRST, :], in_=wv[:, 0:W_FIRST, :])
        bias = []
        for h in range(2):
            b_h = const.tile([P, 1], BF16, name="bias%d" % h)
            nc.sync.dma_start(out=b_h[:], in_=bi[128 * h:128 * (h + 1)].rearrange("(p o) -> p o", o=1))
            bias.append(b_h)
        load_chunk(2)
        nc.sync.dma_start(out=w_all[:, W_FIRST:NV, :], in_=wv[:, W_FIRST:NV, :])

        ident = const.tile([P, P], F32)
        make_identity(nc, ident[:])
        ident_bf = const.tile([P, P], BF16)
        make_identity(nc, ident_bf[:])
        zcol = const.tile([P, 1], F32)
        x_t = []
        for h in range(2):
            t_h = const.tile([P, XR, BLK], F32, name="x_t%d" % h)
            nc.gpsimd.memset(t_h[:, :, 0:BLK:BLK - 1], 0.0)
            x_t.append(t_h)
        xp = const.tile([P, 3, XL], F32)
        nc.gpsimd.memset(xp[:, :, 0:F], 0.0)
        zblk = const.tile([P, F], F32)
        nc.gpsimd.memset(zblk[:], 0.0)
        out_keep = const.tile([P, NV * F + NV // 4], F32)
        pm = out_keep[:, NV * F:NV * F + NV // 4]
        msum = const.tile([P, 2], F32)
        nc.vector.tensor_reduce(out=msum[:, 0:1], in_=ident[:, 0:P:32], axis=AX.X, op=ALU.add)
        nc.vector.tensor_reduce(out=msum[:, 1:2], in_=ident[:, 31:P:32], axis=AX.X, op=ALU.add)
        mask = const.tile([P, 2], F32)
        nc.vector.tensor_scalar(out=mask[:], in0=msum[:], scalar1=-1.0, scalar2=1.0, op0=ALU.mult, op1=ALU.add)

        wi_grp = const.tile([P, 2, F, 4], BF16, align_bytes=64)
        nc.vector.tensor_copy(out=wi_grp[:], in_=wi_raw[:].rearrange("p g j c -> p g c j"))
        wi_codes = const.tile([P, 2 * F], U32, align_bytes=64)
        wi_scales = const.tile([P, 2 * F], U8, align_bytes=64)
        nc.vector.quantize_mx(
            out=wi_codes[:].bitcast(FP8X4),
            scales=wi_scales[:],
            in_=wi_grp[:].rearrange("p g c j -> p (g c j)"),
        )

        grps = {}

        def turn(k, r):
            nv = CHUNKS[k][1]
            if r == 0:
                grp_new = gpool.tile([P, 2, nv * P, 2], F32, tag="grp", name="grp", align_bytes=64)
                grps[k] = grp_new
                if k + 2 < len(CHUNKS) and k >= 1:
                    load_chunk(k + 2)
            grp = grps[k]
            words = xtiles[k][:, r, :].bitcast(F32)
            xt = psx.tile([P, 2, 2, P], F32, tag="xt", name="xt")
            for g in range(2):
                for u in range(2):
                    nc.tensor.transpose(xt[:, g, u, :], words[:, 256 * g + u:256 * (g + 1):2], ident[:])
            nc.scalar.copy(out=grp[:, :, r * P:(r + 1) * P, :], in_=xt[:].rearrange("p g u r -> p g r u"))

        def project(k):
            v0, nv = CHUNKS[k]
            n = nv * P
            codes = cpool.tile([P, 2 * n], U32, tag="codes", name="codes", align_bytes=64)
            scal = cpool.tile([P, 2 * n], U8, tag="scal", name="scal", align_bytes=64)
            nc.vector.quantize_mx(
                out=codes[:].bitcast(FP8X4),
                scales=scal[:],
                in_=grps[k][:].rearrange("p g r u -> p (g r u)").bitcast(BF16),
            )
            s0 = v0 % XR
            for h in range(2):
                acc = psa.tile([P, n], F32, tag="acc", name="acc")
                for g in range(2):
                    wc = slice(g * F + h * P, g * F + (h + 1) * P)
                    xc = slice(g * n, (g + 1) * n)
                    nc.tensor.matmul_mx(
                        out=acc[:],
                        lhsT=wi_codes[:, wc].bitcast(FP8X4),
                        lhsT_scale=wi_scales[:, wc],
                        rhs=codes[:, xc].bitcast(FP8X4),
                        rhs_scale=scal[:, xc],
                        start=(g == 0),
                        stop=(g == 1),
                    )
                nc.scalar.activation(out=x_t[h][:, s0:s0 + nv, 1:1 + P], in_=acc[:].rearrange("p (s e) -> p s e", e=P),
                                     func=ACT.Identity, bias=bias[h][:, 0:1])

        steps = []
        for k in range(4):
            steps.extend([(0, k, r) for r in range(CHUNKS[k][1])])
            steps.append((1, k, 0))
        for k in range(4, len(CHUNKS), 2):
            for kk in (k, k + 1):
                steps.extend([(0, kk, r) for r in range(CHUNKS[kk][1])])
            steps.append((1, k, 0))
            steps.append((1, k + 1, 0))
        turned = {}
        projected = {}
        for n, step in enumerate(steps):
            v0, nv = CHUNKS[step[1]]
            if step[0] == 0:
                turned[v0 + step[2]] = n + 1
            else:
                for r in range(nv):
                    projected[v0 + r] = n + 1
        done = [0]

        def run_to(goal):
            while done[0] < goal:
                kind, k, r = steps[done[0]]
                if kind == 0:
                    turn(k, r)
                else:
                    project(k)
                done[0] += 1

        def slots_of(v2):
            found = []
            for v in (v2 - 2, v2 - 1, v2):
                if 0 <= v < NV:
                    s = v % R + v2 - v
                    if s not in found:
                        found.append(s)
            return found

        def block(i, s):
            return xp[:, i, F * s:F * (s + 1)]

        def to_pixels(vp, i):
            pt = pst.tile([P, F], F32, tag="pt%d" % i, name="pt%d" % i)
            for h in range(2):
                nc.tensor.transpose(pt[:, h * P:(h + 1) * P], x_t[h][:, vp % XR, i:i + P], ident[:])
            for s in slots_of(vp + 1):
                if i == 1:
                    nc.scalar.copy(out=block(1, s), in_=pt[:])
                else:
                    nc.scalar.activation(out=block(i, s), in_=pt[:], func=ACT.Copy, scale=mask[:, i // 2:i // 2 + 1])

        wtiles = {}
        gated = {}
        junk = const.tile([P, 8], F32)

        def meet(chunks, last_col, next_col):
            n_meet = len(gated)
            nc.vector.tensor_copy(out=junk[:, 2 * n_meet:2 * n_meet + 2], in_=prods[last_col][:, 0:2])
            run_to(projected[chunks])
            w_gate = const.tile([P, Q], BF16, name="w_gate%d" % next_col)
            nc.vector.tensor_copy(out=w_gate[:], in_=w_all[:, next_col, :])
            gated[next_col] = w_gate[:]

        prods = {}
        finished = []

        def weights(v):
            wps = psw.tile([P, Q], F32, tag="wps", name="wps")
            nc.tensor.matmul(out=wps[:], lhsT=ident_bf[:], rhs=w_all[:, v, :], start=True, stop=True)
            wtiles[v] = wps

        def involve(v):
            b0 = F * (v % R)
            prod = ppool.tile([P, FLAT], F32, tag="prod", name="prod")
            if v in V_COLS:
                nc.vector.tensor_tensor(
                    out=prod[:].rearrange("p (a f) -> p a f", a=3),
                    in0=xp[:, :, b0:b0 + 3 * F],
                    in1=wtiles[v][:].rearrange("p (g m) -> p g m", m=9).unsqueeze(2).to_broadcast([P, 16, 16, 9]),
                    op=ALU.mult,
                )
            else:
                nc.gpsimd.tensor_tensor(
                    out=prod[:].rearrange("p (a f) -> p a f", a=3),
                    in0=xp[:, :, b0:b0 + 3 * F],
                    in1=gated.get(v, w_all[:, v, :]).rearrange("p (g m) -> p g m", m=9).unsqueeze(2).to_broadcast([P, 16, 16, 9]),
                    op=ALU.mult,
                )
            prods[v] = prod

        def reduce_nine(v):
            nc.vector.tensor_reduce(
                out=out_keep[:, F * v:F * (v + 1)],
                in_=prods[v][:].rearrange("p (o m) -> p o m", m=9),
                axis=AX.X,
                op=ALU.add,
            )

        def finish(v, n):
            col = len(finished)
            finished.append(v)
            nc.vector.tensor_reduce(out=pm[:, col:col + 1], in_=out_keep[:, F * v:F * (v + n)], axis=AX.X,
                                    op=ALU.max, apply_absolute_value=True)
            nc.sync.dma_start(out=o0[:, v:v + n, :], in_=out_keep[:, F * v:F * (v + n)].rearrange("p (v c) -> p v c", c=F))

        run_to(turned[0])
        keep_warm(1)
        run_to(projected[0])
        keep_warm(1)
        run_to(turned[1])
        keep_warm(1)
        run_to(projected[1])
        keep_warm(1)
        for vp, i in ((0, 0), (0, 1), (0, 2)):
            to_pixels(vp, i)
        keep_warm(1)
        nc.scalar.copy(out=zcol[:], in_=warm[:, 0:1])
        for vp, i in ((1, 0), (1, 1), (1, 2)):
            to_pixels(vp, i)
        weights(V_COLS[0])
        run_to(projected[3])
        for i in (0, 1, 2):
            to_pixels(2, i)

        def summed(c):
            reduce_nine(c)
            if c % 4 == 0 and c >= 4:
                finish(c - 4, 4)
            if c == NV - 2:
                finish(NV - 4, 3)

        for v in range(NV + LAG):
            if v == 0:
                run_to(turned[7])
            elif v < 4:
                run_to(turned[9 + 2 * v])
            elif v + 12 < NV and v != 12:
                run_to(turned[v + 12])
            if v > 0 and v + 1 + LOOK < NV:
                for i in (0, 1, 2):
                    to_pixels(v + 1 + LOOK, i)
            if v == NV - 4:
                for s in slots_of(NV + 1):
                    nc.scalar.copy(out=xp[:, :, F * s:F * (s + 1)], in_=zblk[:].unsqueeze(1).to_broadcast([P, 3, F]))
            if v >= LAG and v - LAG > 0:
                summed(v - LAG)
            if v < NV and v in V_COLS:
                involve(v)
                if V_COLS.index(v) + 1 < NVC:
                    weights(V_COLS[V_COLS.index(v) + 1])
            if v in MEETS:
                meet(*MEETS[v])
            if v + 1 < NV and v + 1 not in V_COLS:
                involve(v + 1)
            if v == 0:
                for i in (0, 1, 2):
                    to_pixels(1 + LOOK, i)
                summed(0)
                run_to(projected[7])
                run_to(turned[9])

        nc.sync.dma_start(out=o0[:, NV - 1, :], in_=out_keep[:, F * (NV - 1):F * NV])
        pmax = const.tile([P, 1], F32)
        nc.vector.tensor_reduce(out=pmax[:], in_=out_keep[:, F * (NV - 1):NV * F + NV // 4], axis=AX.X,
                                op=ALU.max, apply_absolute_value=True)
        spread = psx.tile([P, P], F32, tag="xt", name="spread")
        nc.tensor.transpose(spread[:], pmax[:, 0:1].to_broadcast([P, P]), ident[:])
        scaled = const.tile([P, P], F32)
        step_size = const.tile([P, 1], F32)
        nc.vector.tensor_scalar(out=scaled[:], in0=spread[:], scalar1=1.0 / 448.0, scalar2=None, op0=ALU.mult, op1=ALU.max,
                                accum_out=step_size[:])
        fac = const.tile([P, 1], F32)
        nc.vector.reciprocal(out=fac[:], in_=step_size[:])

        for piece in range(8):
            f8 = fpool.tile([P, 1024], FP8, tag="f8", name="f8")
            for sub in range(2):
                a = 512 * sub
                b = 1024 * piece + a
                if (2 * piece + sub) % 8 in S_SUBS:
                    nc.scalar.activation(out=f8[:, a:a + 512], in_=out_keep[:, b:b + 512], func=ACT.Identity,
                                         scale=fac[:, 0:1], bias=zcol[:, 0:1], saturate=False)
                else:
                    nc.vector.tensor_scalar(out=f8[:, a:a + 512], in0=out_keep[:, b:b + 512], scalar1=fac[:, 0:1],
                                            scalar2=None, op0=ALU.mult, saturate=False)
            nc.sync.dma_start(out=o1[:, 1024 * piece:1024 * (piece + 1)], in_=f8[:].bitcast(U8))
